import numpy as np
import ml_dtypes


def mxq(x, axis, fmt="e4m3"):
    dtype, down = {"e4m3": (ml_dtypes.float8_e4m3fn, 7), "e5m2": (ml_dtypes.float8_e5m2, 14)}[fmt]
    v = np.moveaxis(np.asarray(x, np.float32).astype(ml_dtypes.bfloat16).astype(np.float64), axis, -1)
    blocks = v.reshape(v.shape[:-1] + (-1, 32))
    amax = np.abs(blocks).max(-1, keepdims=True)
    byte = np.maximum(np.where(amax > 0, np.frexp(amax)[1] - 1 + 127, 0) - down, 1)
    scale = np.exp2(byte - 127.0)
    codes = (blocks / scale).astype(np.float32).astype(dtype).astype(np.float64)
    return np.moveaxis((codes * scale).reshape(v.shape), -1, axis)


WIDE = False


def mx_kscale(k):
    if not WIDE:
        return np.ones(k)
    levels = np.array([10, -10, 5, -5, 0])
    a = np.random.permutation(np.resize(levels, k // 512 * 4)).reshape(k // 512, 4)
    idx = np.arange(k)
    return np.exp2(a[idx // 512, idx % 128 // 32])


BF16 = ml_dtypes.bfloat16


def bf(x):
    return np.asarray(x, np.float32).astype(BF16)


def f64(x):
    return np.asarray(x).astype(np.float64)


B, S, H, NH, FF = 8, 512, 1024, 8, 1024
EPS = 1e-7


def layer_norm(x, g, b):
    m = x.mean(-1, keepdims=True)
    v = ((x - m) ** 2).mean(-1, keepdims=True)
    return (x - m) / np.sqrt(v + EPS) * g + b


def setup_inputs():
    s = mx_kscale(FF)
    r = np.random.standard_normal
    return {"ff": bf(r((B, S, FF)) * 0.65 * s), "attn_out": bf(r((B, S, H))),
            "Wf": bf(r((FF, H)) * 1.5 / np.sqrt(FF) / s[:, None]), "b_f": bf(r(H) * 0.2),
            "ln2_g": bf(1.0 + 0.1 * r(H)), "ln2_b": bf(0.1 * r(H))}


def reference(ff, attn_out, Wf, b_f, ln2_g, ln2_b):
    u = (mxq(f64(ff), 2, "e4m3") @ mxq(f64(Wf), 0, "e4m3")) + f64(b_f) + f64(attn_out)
    return layer_norm(u, f64(ln2_g), f64(ln2_b))

@@ -1,0 +1,200 @@
+from contextlib import ExitStack
+
+import concourse.mybir as mybir
+from concourse.masks import make_identity
+
+F32 = mybir.dt.float32
+BF16 = mybir.dt.bfloat16
+U32 = mybir.dt.uint32
+U8 = mybir.dt.uint8
+FP8X4 = mybir.dt.float8_e4m3fn_x4
+ALU = mybir.AluOpType
+ACT = mybir.ActivationFunctionType
+
+P = 128
+PACK = 4
+K_PASS = P * PACK
+BATCH, SEQ, K, H = 8, 512, 1024, 1024
+PASSES = K // K_PASS
+TILES = SEQ // P
+BANK = 512
+HALVES = H // BANK
+EPS = 1e-7
+
+FLOPS = 2 * BATCH * SEQ * K * H
+
+
+def tile_disentangledattention_pc_t_kernel(tc, ff, attn_out, Wf, b_f, ln2_g, ln2_b, out):
+    nc = tc.nc
+    ff_v = ff.rearrange("b (p j) f -> b p j f", j=TILES)
+    res_v = attn_out.rearrange("b (p j) f -> b p j f", j=TILES)
+    out_v = out.rearrange("b (p j) f -> b p j f", j=TILES)
+    w_v = Wf.rearrange("(c q e) n -> c q e n", q=P, e=2)
+
+    with ExitStack() as ctx:
+        const = ctx.enter_context(tc.tile_pool(name="const", bufs=1))
+        weights = ctx.enter_context(tc.tile_pool(name="weights", bufs=1))
+        loads = ctx.enter_context(tc.tile_pool(name="loads", bufs=3))
+        quant = ctx.enter_context(tc.tile_pool(name="quant", bufs=2))
+        work = ctx.enter_context(tc.tile_pool(name="work", bufs=3))
+        stats = ctx.enter_context(tc.tile_pool(name="stats", bufs=4))
+        psum_const = ctx.enter_context(tc.psum_pool(name="psum_const", bufs=1))
+        psum_t = ctx.enter_context(tc.psum_pool(name="psum_t", bufs=2))
+        psum_acc = ctx.enter_context(tc.psum_pool(name="psum_acc", bufs=4))
+
+        def half(h):
+            return slice(h * BANK, (h + 1) * BANK)
+
+        ident = const.tile([P, P], F32)
+        make_identity(nc, ident[:])
+        ones = const.tile([P, P], BF16)
+        nc.vector.memset(ones[:], 1.0)
+        eps_t = const.tile([P, 1], F32)
+        nc.vector.memset(eps_t[:], EPS)
+        warm = const.tile([P, 1], F32)
+        nc.scalar.activation(out=warm[:], in_=eps_t[:], func=ACT.Sqrt)
+
+        rows = const.tile([P, 3, H], BF16)
+        nc.vector.memset(rows[:], 0.0)
+        for v, vec in enumerate((b_f, ln2_g, ln2_b)):
+            nc.scalar.dma_start(out=rows[0:1, v, :], in_=vec.rearrange("(o n) -> o n", o=1))
+
+        def load(b):
+            ff_sb = loads.tile([P, TILES, K], BF16)
+            nc.sync.dma_start(out=ff_sb[:], in_=ff_v[b])
+            res_sb = loads.tile([P, TILES, H], BF16)
+            nc.sync.dma_start(out=res_sb[:], in_=res_v[b])
+            return ff_sb, res_sb
+
+        ff_tiles = {}
+        res_tiles = {}
+        ff_tiles[0] = loads.tile([P, TILES, K], BF16, name="ff_sb")
+        nc.sync.dma_start(out=ff_tiles[0][:], in_=ff_v[0])
+        w_raw = weights.tile([P, PASSES, PACK, H], BF16)
+        for g in range(PASSES):
+            for u2 in range(2):
+                nc.sync.dma_start(out=w_raw[:, g, 2 * u2 : 2 * u2 + 2, :], in_=w_v[2 * g + u2])
+        res_tiles[0] = loads.tile([P, TILES, H], BF16, name="res_sb")
+        nc.sync.dma_start(out=res_tiles[0][:], in_=res_v[0])
+        ff_tiles[1], res_tiles[1] = load(1)
+
+        gain_ps = psum_const.tile([P, H], BF16)
+        shift_ps = psum_const.tile([P, H], BF16)
+        bias_bc = const.tile([P, H], BF16)
+        for h in range(HALVES):
+            nc.tensor.matmul(out=gain_ps[:, half(h)], lhsT=ones[:], rhs=rows[:, 1, half(h)], start=True, stop=True)
+            nc.tensor.matmul(out=shift_ps[:, half(h)], lhsT=ones[:], rhs=rows[:, 2, half(h)], start=True, stop=True)
+            bias_ps = psum_acc.tile([P, BANK], F32, name="acc")
+            nc.tensor.matmul(out=bias_ps[:], lhsT=ones[:], rhs=rows[:, 0, half(h)], start=True, stop=True)
+            nc.vector.tensor_copy(out=bias_bc[:, half(h)], in_=bias_ps[:])
+
+        def transpose_tile(ff_sb, grouped, j):
+            words = ff_sb[:, j, :].bitcast(F32)
+            xt = psum_t.tile([P, PASSES * 2, P], F32)
+            for c in range(PASSES * 2):
+                nc.tensor.transpose(xt[:, c, :], words[:, c * P : (c + 1) * P], ident[:])
+            nc.scalar.copy(
+                out=grouped[:, j].bitcast(F32),
+                in_=xt[:].rearrange("p (g u) r -> p g r u", u=2),
+            )
+
+        def quantise_ff(grouped):
+            ff_codes = quant.tile([P, TILES * PASSES * P], U32, align_bytes=64)
+            ff_scales = quant.tile([P, TILES * PASSES * P], U8, align_bytes=64)
+            nc.vector.quantize_mx(
+                out=ff_codes[:].bitcast(FP8X4),
+                scales=ff_scales[:],
+                in_=grouped[:].rearrange("p j g r t -> p (j g r t)"),
+            )
+            return ff_codes, ff_scales
+
+        grouped_tiles = {}
+        grouped_tiles[0] = quant.tile([P, TILES, PASSES, P, PACK], BF16, align_bytes=64, name="grouped")
+        for j in range(TILES):
+            transpose_tile(ff_tiles[0], grouped_tiles[0], j)
+
+        w_grp = weights.tile([P, PASSES, H, PACK], BF16, align_bytes=64)
+        w_codes = weights.tile([P, PASSES, H], U32, align_bytes=64)
+        w_scales = weights.tile([P, PASSES, H], U8, align_bytes=64)
+
+        def regroup_w(copy, g, h):
+            copy(
+                out=w_grp[:, g, half(h), :].rearrange("p (c i) t -> p c t i", i=4),
+                in_=w_raw[:, g, :, half(h)].rearrange("p t (c i) -> p c t i", i=4),
+            )
+
+        def quantise_w(g, h):
+            nc.vector.quantize_mx(
+                out=w_codes[:, g, half(h)].bitcast(FP8X4),
+                scales=w_scales[:, g, half(h)],
+                in_=w_grp[:, g, half(h), :].rearrange("p n t -> p (n t)"),
+            )
+
+        codes_tiles = {}
+        regroup_w(nc.vector.tensor_copy, 0, 0)
+        regroup_w(nc.scalar.copy, 0, 1)
+        codes_tiles[0] = quantise_ff(grouped_tiles[0])
+        regroup_w(nc.vector.tensor_copy, 1, 0)
+        regroup_w(nc.scalar.copy, 1, 1)
+        for h in range(HALVES):
+            for g in range(PASSES):
+                quantise_w(g, h)
+
+        def add_bias(res_sb, j):
+            rb = work.tile([P, H], F32)
+            for h in range(HALVES):
+                nc.gpsimd.tensor_tensor(out=rb[:, half(h)], in0=res_sb[:, j, half(h)], in1=bias_bc[:, half(h)], op=ALU.add)
+            return rb
+
+        def project_and_add(codes, j, rb):
+            ff_codes, ff_scales = codes
+            u = work.tile([P, H], F32)
+            for h in range(HALVES):
+                acc = psum_acc.tile([P, BANK], F32)
+                for g in range(PASSES):
+                    tok = slice((j * PASSES + g) * P, (j * PASSES + g + 1) * P)
+                    nc.tensor.matmul_mx(
+                        out=acc[:],
+                        lhsT=ff_codes[:, tok].bitcast(FP8X4),
+                        lhsT_scale=ff_scales[:, tok],
+                        rhs=w_codes[:, g, half(h)].bitcast(FP8X4),
+                        rhs_scale=w_scales[:, g, half(h)],
+                        start=(g == 0),
+                        stop=(g == PASSES - 1),
+                    )
+                nc.vector.tensor_tensor(out=u[:, half(h)], in0=acc[:], in1=rb[:, half(h)], op=ALU.add)
+            return u
+
+        def statistics(u):
+            negmean = stats.tile([P, 1], F32)
+            unused_a = stats.tile([P, H], BF16, name="unused")
+            nc.scalar.activation(out=unused_a[:], in_=u[:], func=ACT.Identity, scale=-1.0 / H, accum_out=negmean[:])
+            ssq = stats.tile([P, 1], F32)
+            unused_b = stats.tile([P, H], BF16, name="unused")
+            nc.scalar.activation(out=unused_b[:], in_=u[:], func=ACT.Square, bias=negmean[:], scale=1.0, accum_out=ssq[:])
+            std = stats.tile([P, 1], F32)
+            nc.scalar.activation(out=std[:], in_=ssq[:], func=ACT.Sqrt, bias=eps_t[:], scale=1.0 / H)
+            return negmean, std
+
+        def normalise_and_store(u, negmean, std, b, j):
+            rstd = stats.tile([P, 1], F32)
+            nc.vector.reciprocal(out=rstd[:], in_=std[:])
+            y = work.tile([P, H], F32)
+            nc.vector.scalar_tensor_tensor(out=y[:], in0=u[:], scalar=negmean[:], in1=gain_ps[:], op0=ALU.add, op1=ALU.mult)
+            nc.vector.scalar_tensor_tensor(out=y[:], in0=y[:], scalar=rstd[:], in1=shift_ps[:], op0=ALU.mult, op1=ALU.add)
+            nc.sync.dma_start(out=out_v[b, :, j, :], in_=y[:])
+
+        for b in range(BATCH):
+            if b + 2 < BATCH:
+                ff_tiles[b + 2], res_tiles[b + 2] = load(b + 2)
+            if b + 1 < BATCH:
+                grouped_tiles[b + 1] = quant.tile([P, TILES, PASSES, P, PACK], BF16, align_bytes=64, name="grouped")
+            for j in range(TILES):
+                if b + 1 < BATCH:
+                    transpose_tile(ff_tiles[b + 1], grouped_tiles[b + 1], j)
+                rb = add_bias(res_tiles[b], j)
+                u = project_and_add(codes_tiles[b], j, rb)
+                negmean, std = statistics(u)
+                normalise_and_store(u, negmean, std, b, j)
+            if b + 1 < BATCH:
+                codes_tiles[b + 1] = quantise_ff(grouped_tiles[b + 1])

@@ -14,104 +14,161 @@ ACT = mybir.ActivationFunctionType
 P = 128
 PACK = 4
 K_PASS = P * PACK
-BATCH, SEQ, K, H = 8, 512, 1024, 1024
+TOKENS, K, H = 8 * 512, 1024, 1024
 PASSES = K // K_PASS
-TILES = SEQ // P
+N_TILES = TOKENS // P
+GROUP = 4
 BANK = 512
 HALVES = H // BANK
 EPS = 1e-7
 
-FLOPS = 2 * BATCH * SEQ * K * H
+FLOPS = 2 * TOKENS * K * H
+PREP = GROUP + 2
+FF_AHEAD = PREP + 4
+RES_AHEAD = 4
 
 
 def tile_disentangledattention_pc_t_kernel(tc, ff, attn_out, Wf, b_f, ln2_g, ln2_b, out):
     nc = tc.nc
-    ff_v = ff.rearrange("b (p j) f -> b p j f", j=TILES)
-    res_v = attn_out.rearrange("b (p j) f -> b p j f", j=TILES)
-    out_v = out.rearrange("b (p j) f -> b p j f", j=TILES)
+    ff_v = ff.rearrange("b s f -> (b s) f").rearrange("(i p) f -> i p f", p=P)
+    res_v = attn_out.rearrange("b s f -> (b s) f").rearrange("(i p) f -> i p f", p=P)
+    out_v = out.rearrange("b s f -> (b s) f").rearrange("(i p) f -> i p f", p=P)
     w_v = Wf.rearrange("(c q e) n -> c q e n", q=P, e=2)
 
     with ExitStack() as ctx:
         const = ctx.enter_context(tc.tile_pool(name="const", bufs=1))
         weights = ctx.enter_context(tc.tile_pool(name="weights", bufs=1))
-        loads = ctx.enter_context(tc.tile_pool(name="loads", bufs=3))
+        ff_pool = ctx.enter_context(tc.tile_pool(name="ff_pool", bufs=FF_AHEAD))
+        res_pool = ctx.enter_context(tc.tile_pool(name="res_pool", bufs=RES_AHEAD + 1))
         quant = ctx.enter_context(tc.tile_pool(name="quant", bufs=2))
-        work = ctx.enter_context(tc.tile_pool(name="work", bufs=3))
+        work = ctx.enter_context(tc.tile_pool(name="work", bufs=4))
+        y_pool = ctx.enter_context(tc.tile_pool(name="y_pool", bufs=5))
         stats = ctx.enter_context(tc.tile_pool(name="stats", bufs=4))
         psum_const = ctx.enter_context(tc.psum_pool(name="psum_const", bufs=1))
         psum_t = ctx.enter_context(tc.psum_pool(name="psum_t", bufs=2))
         psum_acc = ctx.enter_context(tc.psum_pool(name="psum_acc", bufs=4))
+        ctx.enter_context(tc.manual_schedule())
 
         def half(h):
             return slice(h * BANK, (h + 1) * BANK)
+
+        ff_sb, res_sb, xt, grouped, codes = {}, {}, {}, {}, {}
+        rb, acc, u, negmean, ssq, std, rstd, y = {}, {}, {}, {}, {}, {}, {}, {}
+
+        def load_ff(i):
+            ff_sb[i] = ff_pool.tile([P, K], BF16, name="ff_sb")
+            nc.sync.dma_start(out=ff_sb[i][:], in_=ff_v[i])
+
+        def load_res(i):
+            res_sb[i] = res_pool.tile([P, H], BF16, name="res_sb")
+            nc.sync.dma_start(out=res_sb[i][:], in_=res_v[i])
+
+        def transpose(i):
+            words = ff_sb[i][:].bitcast(F32)
+            xt[i] = psum_t.tile([P, PASSES * 2, P], F32, name="xt")
+            for c in range(PASSES * 2):
+                nc.tensor.transpose(xt[i][:, c, :], words[:, c * P : (c + 1) * P], ident[:])
+
+        def regroup(i):
+            if i % GROUP == 0:
+                grouped[i // GROUP] = quant.tile([P, GROUP, PASSES, P, PACK], BF16, align_bytes=64, name="grouped")
+            nc.scalar.copy(
+                out=grouped[i // GROUP][:, i % GROUP].bitcast(F32),
+                in_=xt[i][:].rearrange("p (g u) r -> p g r u", u=2),
+            )
+
+        def quantise_ff(n):
+            ff_codes = quant.tile([P, GROUP * PASSES * P], U32, align_bytes=64)
+            ff_scales = quant.tile([P, GROUP * PASSES * P], U8, align_bytes=64)
+            nc.vector.quantize_mx(
+                out=ff_codes[:].bitcast(FP8X4),
+                scales=ff_scales[:],
+                in_=grouped[n][:].rearrange("p j g r t -> p (j g r t)"),
+            )
+            codes[n] = (ff_codes, ff_scales)
+
+        def add_bias(i):
+            rb[i] = work.tile([P, H], F32, name="rb")
+            for h in range(HALVES):
+                nc.gpsimd.tensor_tensor(out=rb[i][:, half(h)], in0=res_sb[i][:, half(h)], in1=bias_bc[:, half(h)], op=ALU.add)
+
+        def project(i):
+            ff_codes, ff_scales = codes[i // GROUP]
+            for h in range(HALVES):
+                acc[i, h] = psum_acc.tile([P, BANK], F32, name="acc")
+                for g in range(PASSES):
+                    tok = slice(((i % GROUP) * PASSES + g) * P, ((i % GROUP) * PASSES + g + 1) * P)
+                    nc.tensor.matmul_mx(
+                        out=acc[i, h][:],
+                        lhsT=ff_codes[:, tok].bitcast(FP8X4),
+                        lhsT_scale=ff_scales[:, tok],
+                        rhs=w_codes[:, g, half(h)].bitcast(FP8X4),
+                        rhs_scale=w_scales[:, g, half(h)],
+                        start=(g == 0),
+                        stop=(g == PASSES - 1),
+                    )
+
+        def add_residual(i, h):
+            if h == 0:
+                u[i] = work.tile([P, H], F32, name="u")
+            nc.vector.tensor_tensor(out=u[i][:, half(h)], in0=acc[i, h][:], in1=rb[i][:, half(h)], op=ALU.add)
+
+        def mean(i):
+            negmean[i] = stats.tile([P, 1], F32, name="negmean")
+            unused = stats.tile([P, H], BF16, name="unused")
+            nc.scalar.activation(out=unused[:], in_=u[i][:], func=ACT.Identity, scale=-1.0 / H, accum_out=negmean[i][:])
+
+        def squared_deviations(i):
+            ssq[i] = stats.tile([P, 1], F32, name="ssq")
+            unused = stats.tile([P, H], BF16, name="unused")
+            nc.scalar.activation(out=unused[:], in_=u[i][:], func=ACT.Square, bias=negmean[i][:], scale=1.0, accum_out=ssq[i][:])
+
+        def deviation(i):
+            std[i] = stats.tile([P, 1], F32, name="std")
+            nc.scalar.activation(out=std[i][:], in_=ssq[i][:], func=ACT.Sqrt, bias=eps_t[:], scale=1.0 / H)
+
+        def reciprocal(i):
+            rstd[i] = stats.tile([P, 1], F32, name="rstd")
+            nc.vector.reciprocal(out=rstd[i][:], in_=std[i][:])
+
+        def centre_and_gain(i):
+            y[i] = y_pool.tile([P, H], F32, name="y")
+            nc.vector.scalar_tensor_tensor(out=y[i][:], in0=u[i][:], scalar=negmean[i][:], in1=gain_ps[:], op0=ALU.add, op1=ALU.mult)
+
+        def scale_shift_store(i):
+            nc.vector.scalar_tensor_tensor(out=y[i][:], in0=y[i][:], scalar=rstd[i][:], in1=shift_ps[:], op0=ALU.mult, op1=ALU.add)
+            nc.sync.dma_start(out=out_v[i], in_=y[i][:])
 
         ident = const.tile([P, P], F32)
         make_identity(nc, ident[:])
         ones = const.tile([P, P], BF16)
         nc.vector.memset(ones[:], 1.0)
+        rows = const.tile([P, 3, H], BF16)
+        nc.vector.memset(rows[:], 0.0)
         eps_t = const.tile([P, 1], F32)
         nc.vector.memset(eps_t[:], EPS)
         warm = const.tile([P, 1], F32)
         nc.scalar.activation(out=warm[:], in_=eps_t[:], func=ACT.Sqrt)
 
-        rows = const.tile([P, 3, H], BF16)
-        nc.vector.memset(rows[:], 0.0)
-        for v, vec in enumerate((b_f, ln2_g, ln2_b)):
-            nc.scalar.dma_start(out=rows[0:1, v, :], in_=vec.rearrange("(o n) -> o n", o=1))
-
-        def load(b):
-            ff_sb = loads.tile([P, TILES, K], BF16)
-            nc.sync.dma_start(out=ff_sb[:], in_=ff_v[b])
-            res_sb = loads.tile([P, TILES, H], BF16)
-            nc.sync.dma_start(out=res_sb[:], in_=res_v[b])
-            return ff_sb, res_sb
-
-        ff_tiles = {}
-        res_tiles = {}
-        ff_tiles[0] = loads.tile([P, TILES, K], BF16, name="ff_sb")
-        nc.sync.dma_start(out=ff_tiles[0][:], in_=ff_v[0])
         w_raw = weights.tile([P, PASSES, PACK, H], BF16)
-        for g in range(PASSES):
+
+        def load_w(g, h):
             for u2 in range(2):
-                nc.sync.dma_start(out=w_raw[:, g, 2 * u2 : 2 * u2 + 2, :], in_=w_v[2 * g + u2])
-        res_tiles[0] = loads.tile([P, TILES, H], BF16, name="res_sb")
-        nc.sync.dma_start(out=res_tiles[0][:], in_=res_v[0])
-        ff_tiles[1], res_tiles[1] = load(1)
+                nc.sync.dma_start(out=w_raw[:, g, 2 * u2 : 2 * u2 + 2, half(h)], in_=w_v[2 * g + u2][:, :, half(h)])
 
-        gain_ps = psum_const.tile([P, H], BF16)
-        shift_ps = psum_const.tile([P, H], BF16)
-        bias_bc = const.tile([P, H], BF16)
-        for h in range(HALVES):
-            nc.tensor.matmul(out=gain_ps[:, half(h)], lhsT=ones[:], rhs=rows[:, 1, half(h)], start=True, stop=True)
-            nc.tensor.matmul(out=shift_ps[:, half(h)], lhsT=ones[:], rhs=rows[:, 2, half(h)], start=True, stop=True)
-            bias_ps = psum_acc.tile([P, BANK], F32, name="acc")
-            nc.tensor.matmul(out=bias_ps[:], lhsT=ones[:], rhs=rows[:, 0, half(h)], start=True, stop=True)
-            nc.vector.tensor_copy(out=bias_bc[:, half(h)], in_=bias_ps[:])
-
-        def transpose_tile(ff_sb, grouped, j):
-            words = ff_sb[:, j, :].bitcast(F32)
-            xt = psum_t.tile([P, PASSES * 2, P], F32)
-            for c in range(PASSES * 2):
-                nc.tensor.transpose(xt[:, c, :], words[:, c * P : (c + 1) * P], ident[:])
-            nc.scalar.copy(
-                out=grouped[:, j].bitcast(F32),
-                in_=xt[:].rearrange("p (g u) r -> p g r u", u=2),
-            )
-
-        def quantise_ff(grouped):
-            ff_codes = quant.tile([P, TILES * PASSES * P], U32, align_bytes=64)
-            ff_scales = quant.tile([P, TILES * PASSES * P], U8, align_bytes=64)
-            nc.vector.quantize_mx(
-                out=ff_codes[:].bitcast(FP8X4),
-                scales=ff_scales[:],
-                in_=grouped[:].rearrange("p j g r t -> p (j g r t)"),
-            )
-            return ff_codes, ff_scales
-
-        grouped_tiles = {}
-        grouped_tiles[0] = quant.tile([P, TILES, PASSES, P, PACK], BF16, align_bytes=64, name="grouped")
-        for j in range(TILES):
-            transpose_tile(ff_tiles[0], grouped_tiles[0], j)
+        load_w(0, 0)
+        for v, vec in enumerate((b_f, ln2_g, ln2_b)):
+            nc.sync.dma_start(out=rows[0:1, v, :], in_=vec.rearrange("(o n) -> o n", o=1))
+        load_w(1, 0)
+        for i in range(GROUP):
+            load_ff(i)
+        load_res(0)
+        load_w(0, 1)
+        load_w(1, 1)
+        for i in range(1, RES_AHEAD):
+            load_res(i)
+        for i in range(GROUP, FF_AHEAD):
+            load_ff(i)
 
         w_grp = weights.tile([P, PASSES, H, PACK], BF16, align_bytes=64)
         w_codes = weights.tile([P, PASSES, H], U32, align_bytes=64)
@@ -130,71 +187,65 @@ def tile_disentangledattention_pc_t_kernel(tc, ff, attn_out, Wf, b_f, ln2_g, ln2
                 in_=w_grp[:, g, half(h), :].rearrange("p n t -> p (n t)"),
             )
 
-        codes_tiles = {}
         regroup_w(nc.vector.tensor_copy, 0, 0)
-        regroup_w(nc.scalar.copy, 0, 1)
-        codes_tiles[0] = quantise_ff(grouped_tiles[0])
         regroup_w(nc.vector.tensor_copy, 1, 0)
-        regroup_w(nc.scalar.copy, 1, 1)
+        quantise_w(0, 0)
+        quantise_w(1, 0)
+
+        bias_bc = const.tile([P, H], BF16)
         for h in range(HALVES):
-            for g in range(PASSES):
-                quantise_w(g, h)
+            bias_ps = psum_acc.tile([P, BANK], F32, name="acc")
+            nc.tensor.matmul(out=bias_ps[:], lhsT=ones[:], rhs=rows[:, 0, half(h)], start=True, stop=True)
+            nc.scalar.copy(out=bias_bc[:, half(h)], in_=bias_ps[:])
+        add_bias(0)
 
-        def add_bias(res_sb, j):
-            rb = work.tile([P, H], F32)
-            for h in range(HALVES):
-                nc.gpsimd.tensor_tensor(out=rb[:, half(h)], in0=res_sb[:, j, half(h)], in1=bias_bc[:, half(h)], op=ALU.add)
-            return rb
+        for i in range(GROUP):
+            transpose(i)
+            regroup(i)
+        quantise_ff(0)
+        regroup_w(nc.vector.tensor_copy, 0, 1)
+        regroup_w(nc.scalar.copy, 1, 1)
+        quantise_w(0, 1)
+        quantise_w(1, 1)
+        for i in range(GROUP, PREP):
+            transpose(i)
+            regroup(i)
 
-        def project_and_add(codes, j, rb):
-            ff_codes, ff_scales = codes
-            u = work.tile([P, H], F32)
-            for h in range(HALVES):
-                acc = psum_acc.tile([P, BANK], F32)
-                for g in range(PASSES):
-                    tok = slice((j * PASSES + g) * P, (j * PASSES + g + 1) * P)
-                    nc.tensor.matmul_mx(
-                        out=acc[:],
-                        lhsT=ff_codes[:, tok].bitcast(FP8X4),
-                        lhsT_scale=ff_scales[:, tok],
-                        rhs=w_codes[:, g, half(h)].bitcast(FP8X4),
-                        rhs_scale=w_scales[:, g, half(h)],
-                        start=(g == 0),
-                        stop=(g == PASSES - 1),
-                    )
-                nc.vector.tensor_tensor(out=u[:, half(h)], in0=acc[:], in1=rb[:, half(h)], op=ALU.add)
-            return u
+        gain_ps = psum_const.tile([P, H], BF16)
+        shift_ps = psum_const.tile([P, H], BF16)
+        for h in range(HALVES):
+            nc.tensor.matmul(out=gain_ps[:, half(h)], lhsT=ones[:], rhs=rows[:, 1, half(h)], start=True, stop=True)
+            nc.tensor.matmul(out=shift_ps[:, half(h)], lhsT=ones[:], rhs=rows[:, 2, half(h)], start=True, stop=True)
 
-        def statistics(u):
-            negmean = stats.tile([P, 1], F32)
-            unused_a = stats.tile([P, H], BF16, name="unused")
-            nc.scalar.activation(out=unused_a[:], in_=u[:], func=ACT.Identity, scale=-1.0 / H, accum_out=negmean[:])
-            ssq = stats.tile([P, 1], F32)
-            unused_b = stats.tile([P, H], BF16, name="unused")
-            nc.scalar.activation(out=unused_b[:], in_=u[:], func=ACT.Square, bias=negmean[:], scale=1.0, accum_out=ssq[:])
-            std = stats.tile([P, 1], F32)
-            nc.scalar.activation(out=std[:], in_=ssq[:], func=ACT.Sqrt, bias=eps_t[:], scale=1.0 / H)
-            return negmean, std
+        def tile_exists(i):
+            return 0 <= i < N_TILES
 
-        def normalise_and_store(u, negmean, std, b, j):
-            rstd = stats.tile([P, 1], F32)
-            nc.vector.reciprocal(out=rstd[:], in_=std[:])
-            y = work.tile([P, H], F32)
-            nc.vector.scalar_tensor_tensor(out=y[:], in0=u[:], scalar=negmean[:], in1=gain_ps[:], op0=ALU.add, op1=ALU.mult)
-            nc.vector.scalar_tensor_tensor(out=y[:], in0=y[:], scalar=rstd[:], in1=shift_ps[:], op0=ALU.mult, op1=ALU.add)
-            nc.sync.dma_start(out=out_v[b, :, j, :], in_=y[:])
-
-        for b in range(BATCH):
-            if b + 2 < BATCH:
-                ff_tiles[b + 2], res_tiles[b + 2] = load(b + 2)
-            if b + 1 < BATCH:
-                grouped_tiles[b + 1] = quant.tile([P, TILES, PASSES, P, PACK], BF16, align_bytes=64, name="grouped")
-            for j in range(TILES):
-                if b + 1 < BATCH:
-                    transpose_tile(ff_tiles[b + 1], grouped_tiles[b + 1], j)
-                rb = add_bias(res_tiles[b], j)
-                u = project_and_add(codes_tiles[b], j, rb)
-                negmean, std = statistics(u)
-                normalise_and_store(u, negmean, std, b, j)
-            if b + 1 < BATCH:
-                codes_tiles[b + 1] = quantise_ff(grouped_tiles[b + 1])
+        for i in range(N_TILES + 3):
+            if tile_exists(i + FF_AHEAD):
+                load_ff(i + FF_AHEAD)
+            if tile_exists(i + RES_AHEAD):
+                load_res(i + RES_AHEAD)
+            if tile_exists(i + 1):
+                add_bias(i + 1)
+            if tile_exists(i + PREP):
+                transpose(i + PREP)
+            if tile_exists(i):
+                project(i)
+                add_residual(i, 0)
+            if tile_exists(i - 2):
+                centre_and_gain(i - 2)
+            if tile_exists(i - 3):
+                reciprocal(i - 3)
+            if tile_exists(i):
+                add_residual(i, 1)
+                mean(i)
+            if tile_exists(i - 1):
+                deviation(i - 1)
+            if tile_exists(i + PREP):
+                regroup(i + PREP)
+            if tile_exists(i):
+                squared_deviations(i)
+            if tile_exists(i - 3):
+                scale_shift_store(i - 3)
+            if i % GROUP == GROUP - 2 and tile_exists(i + 2):
+                quantise_ff((i + 2) // GROUP)

@@ -227,10 +227,12 @@ def tile_disentangledattention_pc_t_kernel(tc, ff, attn_out, Wf, b_f, ln2_g, ln2
                 load_res(i + RES_AHEAD)
             if tile_exists(i + 1):
                 add_bias(i + 1)
-            if tile_exists(i + PREP):
-                transpose(i + PREP)
             if tile_exists(i):
                 project(i)
+            if tile_exists(i + PREP):
+                transpose(i + PREP)
+                regroup(i + PREP)
+            if tile_exists(i):
                 add_residual(i, 0)
             if tile_exists(i - 2):
                 centre_and_gain(i - 2)
@@ -241,8 +243,6 @@ def tile_disentangledattention_pc_t_kernel(tc, ff, attn_out, Wf, b_f, ln2_g, ln2
                 mean(i)
             if tile_exists(i - 1):
                 deviation(i - 1)
-            if tile_exists(i + PREP):
-                regroup(i + PREP)
             if tile_exists(i):
                 squared_deviations(i)
             if tile_exists(i - 3):

@@ -5,6 +5,7 @@ from concourse.masks import make_identity
 
 F32 = mybir.dt.float32
 BF16 = mybir.dt.bfloat16
+I32 = mybir.dt.int32
 U32 = mybir.dt.uint32
 U8 = mybir.dt.uint8
 FP8X4 = mybir.dt.float8_e4m3fn_x4
@@ -26,6 +27,7 @@ FLOPS = 2 * TOKENS * K * H
 PREP = GROUP + 2
 FF_AHEAD = PREP + 4
 RES_AHEAD = 4
+HAND_OVER = 4
 
 
 def tile_disentangledattention_pc_t_kernel(tc, ff, attn_out, Wf, b_f, ln2_g, ln2_b, out):
@@ -42,7 +44,7 @@ def tile_disentangledattention_pc_t_kernel(tc, ff, attn_out, Wf, b_f, ln2_g, ln2
         res_pool = ctx.enter_context(tc.tile_pool(name="res_pool", bufs=RES_AHEAD + 1))
         quant = ctx.enter_context(tc.tile_pool(name="quant", bufs=2))
         work = ctx.enter_context(tc.tile_pool(name="work", bufs=4))
-        y_pool = ctx.enter_context(tc.tile_pool(name="y_pool", bufs=5))
+        y_pool = ctx.enter_context(tc.tile_pool(name="y_pool", bufs=6))
         stats = ctx.enter_context(tc.tile_pool(name="stats", bufs=4))
         psum_const = ctx.enter_context(tc.psum_pool(name="psum_const", bufs=1))
         psum_t = ctx.enter_context(tc.psum_pool(name="psum_t", bufs=2))
@@ -53,7 +55,7 @@ def tile_disentangledattention_pc_t_kernel(tc, ff, attn_out, Wf, b_f, ln2_g, ln2
             return slice(h * BANK, (h + 1) * BANK)
 
         ff_sb, res_sb, xt, grouped, codes = {}, {}, {}, {}, {}
-        rb, acc, u, negmean, ssq, std, rstd, y = {}, {}, {}, {}, {}, {}, {}, {}
+        rb, acc, u, negmean, ssq, rstd, y = {}, {}, {}, {}, {}, {}, {}
 
         def load_ff(i):
             ff_sb[i] = ff_pool.tile([P, K], BF16, name="ff_sb")
@@ -89,8 +91,7 @@ def tile_disentangledattention_pc_t_kernel(tc, ff, attn_out, Wf, b_f, ln2_g, ln2
 
         def add_bias(i):
             rb[i] = work.tile([P, H], F32, name="rb")
-            for h in range(HALVES):
-                nc.gpsimd.tensor_tensor(out=rb[i][:, half(h)], in0=res_sb[i][:, half(h)], in1=bias_bc[:, half(h)], op=ALU.add)
+            nc.gpsimd.tensor_tensor(out=rb[i][:], in0=res_sb[i][:], in1=bias_bc[:], op=ALU.add)
 
         def project(i):
             ff_codes, ff_scales = codes[i // GROUP]
@@ -123,32 +124,44 @@ def tile_disentangledattention_pc_t_kernel(tc, ff, attn_out, Wf, b_f, ln2_g, ln2
             unused = stats.tile([P, H], BF16, name="unused")
             nc.scalar.activation(out=unused[:], in_=u[i][:], func=ACT.Square, bias=negmean[i][:], scale=1.0, accum_out=ssq[i][:])
 
-        def deviation(i):
-            std[i] = stats.tile([P, 1], F32, name="std")
-            nc.scalar.activation(out=std[i][:], in_=ssq[i][:], func=ACT.Sqrt, bias=eps_t[:], scale=1.0 / H)
-
-        def reciprocal(i):
+        def inverse_deviation(i):
             rstd[i] = stats.tile([P, 1], F32, name="rstd")
-            nc.vector.reciprocal(out=rstd[i][:], in_=std[i][:])
+            nc.scalar.activation(out=rstd[i][:], in_=ssq[i][:], func=ACT.Abs_reciprocal_sqrt, bias=eps_t[:], scale=1.0 / H)
 
         def centre_and_gain(i):
             y[i] = y_pool.tile([P, H], F32, name="y")
             nc.vector.scalar_tensor_tensor(out=y[i][:], in0=u[i][:], scalar=negmean[i][:], in1=gain_ps[:], op0=ALU.add, op1=ALU.mult)
 
-        def scale_shift_store(i):
+        def scale_and_shift(i):
             nc.vector.scalar_tensor_tensor(out=y[i][:], in0=y[i][:], scalar=rstd[i][:], in1=shift_ps[:], op0=ALU.mult, op1=ALU.add)
+
+        def scale_only(i):
+            nc.scalar.activation(out=y[i][:], in_=y[i][:], func=ACT.Copy, scale=rstd[i][:])
+
+        def shift_only(i):
+            nc.gpsimd.tensor_tensor(out=y[i][:], in0=y[i][:], in1=shift_bc[:], op=ALU.add)
+
+        def store(i):
             nc.sync.dma_start(out=out_v[i], in_=y[i][:])
 
         ident = const.tile([P, P], F32)
         make_identity(nc, ident[:])
         ones = const.tile([P, P], BF16)
         nc.vector.memset(ones[:], 1.0)
-        rows = const.tile([P, 3, H], BF16)
-        nc.vector.memset(rows[:], 0.0)
+        rows = {}
+        for name in ("bias", "gain", "shift"):
+            rows[name] = const.tile([P, H], BF16, name="row_" + name)
+            nc.vector.memset(rows[name][:].bitcast(I32), 0)
         eps_t = const.tile([P, 1], F32)
         nc.vector.memset(eps_t[:], EPS)
         warm = const.tile([P, 1], F32)
-        nc.scalar.activation(out=warm[:], in_=eps_t[:], func=ACT.Sqrt)
+        nc.scalar.activation(out=warm[:], in_=eps_t[:], func=ACT.Abs_reciprocal_sqrt)
+
+        def load_row(name, vec):
+            nc.sync.dma_start(out=rows[name][0:1, :], in_=vec.rearrange("(o n) -> o n", o=1))
+
+        def spread_row(name, h, out_ps):
+            nc.tensor.matmul(out=out_ps, lhsT=ones[:], rhs=rows[name][:, half(h)], start=True, stop=True)
 
         w_raw = weights.tile([P, PASSES, PACK, H], BF16)
 
@@ -157,25 +170,33 @@ def tile_disentangledattention_pc_t_kernel(tc, ff, attn_out, Wf, b_f, ln2_g, ln2
                 nc.sync.dma_start(out=w_raw[:, g, 2 * u2 : 2 * u2 + 2, half(h)], in_=w_v[2 * g + u2][:, :, half(h)])
 
         load_w(0, 0)
-        for v, vec in enumerate((b_f, ln2_g, ln2_b)):
-            nc.sync.dma_start(out=rows[0:1, v, :], in_=vec.rearrange("(o n) -> o n", o=1))
+        load_row("bias", b_f)
         load_w(1, 0)
-        for i in range(GROUP):
-            load_ff(i)
         load_res(0)
         load_w(0, 1)
         load_w(1, 1)
+        for i in range(GROUP):
+            load_ff(i)
         for i in range(1, RES_AHEAD):
             load_res(i)
+        load_row("gain", ln2_g)
+        load_row("shift", ln2_b)
         for i in range(GROUP, FF_AHEAD):
             load_ff(i)
+
+        bias_bc = const.tile([P, H], BF16)
+        for h in range(HALVES):
+            bias_ps = psum_acc.tile([P, BANK], F32, name="acc")
+            spread_row("bias", h, bias_ps[:])
+            nc.scalar.copy(out=bias_bc[:, half(h)], in_=bias_ps[:])
+        add_bias(0)
 
         w_grp = weights.tile([P, PASSES, H, PACK], BF16, align_bytes=64)
         w_codes = weights.tile([P, PASSES, H], U32, align_bytes=64)
         w_scales = weights.tile([P, PASSES, H], U8, align_bytes=64)
 
-        def regroup_w(copy, g, h):
-            copy(
+        def regroup_w(g, h):
+            nc.vector.tensor_copy(
                 out=w_grp[:, g, half(h), :].rearrange("p (c i) t -> p c t i", i=4),
                 in_=w_raw[:, g, :, half(h)].rearrange("p t (c i) -> p c t i", i=4),
             )
@@ -187,40 +208,36 @@ def tile_disentangledattention_pc_t_kernel(tc, ff, attn_out, Wf, b_f, ln2_g, ln2
                 in_=w_grp[:, g, half(h), :].rearrange("p n t -> p (n t)"),
             )
 
-        regroup_w(nc.vector.tensor_copy, 0, 0)
-        regroup_w(nc.vector.tensor_copy, 1, 0)
-        quantise_w(0, 0)
-        quantise_w(1, 0)
-
-        bias_bc = const.tile([P, H], BF16)
         for h in range(HALVES):
-            bias_ps = psum_acc.tile([P, BANK], F32, name="acc")
-            nc.tensor.matmul(out=bias_ps[:], lhsT=ones[:], rhs=rows[:, 0, half(h)], start=True, stop=True)
-            nc.scalar.copy(out=bias_bc[:, half(h)], in_=bias_ps[:])
-        add_bias(0)
+            for g in range(PASSES):
+                regroup_w(g, h)
+            for g in range(PASSES):
+                quantise_w(g, h)
 
         for i in range(GROUP):
             transpose(i)
             regroup(i)
         quantise_ff(0)
-        regroup_w(nc.vector.tensor_copy, 0, 1)
-        regroup_w(nc.scalar.copy, 1, 1)
-        quantise_w(0, 1)
-        quantise_w(1, 1)
-        for i in range(GROUP, PREP):
-            transpose(i)
-            regroup(i)
 
         gain_ps = psum_const.tile([P, H], BF16)
         shift_ps = psum_const.tile([P, H], BF16)
         for h in range(HALVES):
-            nc.tensor.matmul(out=gain_ps[:, half(h)], lhsT=ones[:], rhs=rows[:, 1, half(h)], start=True, stop=True)
-            nc.tensor.matmul(out=shift_ps[:, half(h)], lhsT=ones[:], rhs=rows[:, 2, half(h)], start=True, stop=True)
+            spread_row("gain", h, gain_ps[:, half(h)])
+            spread_row("shift", h, shift_ps[:, half(h)])
+        shift_bc = const.tile([P, H], BF16)
+        nc.scalar.copy(out=shift_bc[:], in_=shift_ps[:])
+
+        for i in range(GROUP, PREP):
+            transpose(i)
+            regroup(i)
 
         def tile_exists(i):
             return 0 <= i < N_TILES
 
-        for i in range(N_TILES + 3):
+        def handed_over(i):
+            return tile_exists(i) and i % HAND_OVER == 1
+
+        for i in range(N_TILES + 4):
             if tile_exists(i + FF_AHEAD):
                 load_ff(i + FF_AHEAD)
             if tile_exists(i + RES_AHEAD):
@@ -232,20 +249,24 @@ def tile_disentangledattention_pc_t_kernel(tc, ff, attn_out, Wf, b_f, ln2_g, ln2
             if tile_exists(i + PREP):
                 transpose(i + PREP)
                 regroup(i + PREP)
+            if handed_over(i - 3):
+                scale_only(i - 3)
             if tile_exists(i):
                 add_residual(i, 0)
             if tile_exists(i - 2):
                 centre_and_gain(i - 2)
-            if tile_exists(i - 3):
-                reciprocal(i - 3)
             if tile_exists(i):
                 add_residual(i, 1)
                 mean(i)
             if tile_exists(i - 1):
-                deviation(i - 1)
+                inverse_deviation(i - 1)
             if tile_exists(i):
                 squared_deviations(i)
-            if tile_exists(i - 3):
-                scale_shift_store(i - 3)
+            if tile_exists(i - 3) and not handed_over(i - 3):
+                scale_and_shift(i - 3)
+                store(i - 3)
+            if handed_over(i - 4):
+                shift_only(i - 4)
+                store(i - 4)
             if i % GROUP == GROUP - 2 and tile_exists(i + 2):
                 quantise_ff((i + 2) // GROUP)

@@ -79,15 +79,18 @@ def tile_disentangledattention_pc_t_kernel(tc, ff, attn_out, Wf, b_f, ln2_g, ln2
                 in_=xt[i][:].rearrange("p (g u) r -> p g r u", u=2),
             )
 
-        def quantise_ff(n):
-            ff_codes = quant.tile([P, GROUP * PASSES * P], U32, align_bytes=64)
-            ff_scales = quant.tile([P, GROUP * PASSES * P], U8, align_bytes=64)
+        def quantise_ff(n, first, count):
+            if first == 0:
+                ff_codes = quant.tile([P, GROUP * PASSES * P], U32, align_bytes=64)
+                ff_scales = quant.tile([P, GROUP * PASSES * P], U8, align_bytes=64)
+                codes[n] = (ff_codes, ff_scales)
+            ff_codes, ff_scales = codes[n]
+            words = slice(first * PASSES * P, (first + count) * PASSES * P)
             nc.vector.quantize_mx(
-                out=ff_codes[:].bitcast(FP8X4),
-                scales=ff_scales[:],
-                in_=grouped[n][:].rearrange("p j g r t -> p (j g r t)"),
+                out=ff_codes[:, words].bitcast(FP8X4),
+                scales=ff_scales[:, words],
+                in_=grouped[n][:, first : first + count].rearrange("p j g r t -> p (j g r t)"),
             )
-            codes[n] = (ff_codes, ff_scales)
 
         def add_bias(i):
             rb[i] = work.tile([P, H], F32, name="rb")
@@ -132,8 +135,8 @@ def tile_disentangledattention_pc_t_kernel(tc, ff, attn_out, Wf, b_f, ln2_g, ln2
             y[i] = y_pool.tile([P, H], F32, name="y")
             nc.vector.scalar_tensor_tensor(out=y[i][:], in0=u[i][:], scalar=negmean[i][:], in1=gain_ps[:], op0=ALU.add, op1=ALU.mult)
 
-        def scale_and_shift(i):
-            nc.vector.scalar_tensor_tensor(out=y[i][:], in0=y[i][:], scalar=rstd[i][:], in1=shift_ps[:], op0=ALU.mult, op1=ALU.add)
+        def scale_and_shift(i, cols):
+            nc.vector.scalar_tensor_tensor(out=y[i][:, cols], in0=y[i][:, cols], scalar=rstd[i][:], in1=shift_ps[:, cols], op0=ALU.mult, op1=ALU.add)
 
         def scale_only(i):
             nc.scalar.activation(out=y[i][:], in_=y[i][:], func=ACT.Copy, scale=rstd[i][:])
@@ -141,8 +144,8 @@ def tile_disentangledattention_pc_t_kernel(tc, ff, attn_out, Wf, b_f, ln2_g, ln2
         def shift_only(i):
             nc.gpsimd.tensor_tensor(out=y[i][:], in0=y[i][:], in1=shift_bc[:], op=ALU.add)
 
-        def store(i):
-            nc.sync.dma_start(out=out_v[i], in_=y[i][:])
+        def store(i, cols):
+            nc.sync.dma_start(out=out_v[i][:, cols], in_=y[i][:, cols])
 
         ident = const.tile([P, P], F32)
         make_identity(nc, ident[:])
@@ -172,16 +175,14 @@ def tile_disentangledattention_pc_t_kernel(tc, ff, attn_out, Wf, b_f, ln2_g, ln2
         load_w(0, 0)
         load_row("bias", b_f)
         load_w(1, 0)
-        load_res(0)
         load_w(0, 1)
         load_w(1, 1)
-        for i in range(GROUP):
+        for i in range(RES_AHEAD):
             load_ff(i)
-        for i in range(1, RES_AHEAD):
             load_res(i)
         load_row("gain", ln2_g)
         load_row("shift", ln2_b)
-        for i in range(GROUP, FF_AHEAD):
+        for i in range(RES_AHEAD, FF_AHEAD):
             load_ff(i)
 
         bias_bc = const.tile([P, H], BF16)
@@ -217,7 +218,7 @@ def tile_disentangledattention_pc_t_kernel(tc, ff, attn_out, Wf, b_f, ln2_g, ln2
         for i in range(GROUP):
             transpose(i)
             regroup(i)
-        quantise_ff(0)
+            quantise_ff(0, i, 1)
 
         gain_ps = psum_const.tile([P, H], BF16)
         shift_ps = psum_const.tile([P, H], BF16)
@@ -235,7 +236,7 @@ def tile_disentangledattention_pc_t_kernel(tc, ff, attn_out, Wf, b_f, ln2_g, ln2
             return 0 <= i < N_TILES
 
         def handed_over(i):
-            return tile_exists(i) and i % HAND_OVER == 1
+            return tile_exists(i) and i % HAND_OVER == 0
 
         for i in range(N_TILES + 4):
             if tile_exists(i + FF_AHEAD):
@@ -263,10 +264,11 @@ def tile_disentangledattention_pc_t_kernel(tc, ff, attn_out, Wf, b_f, ln2_g, ln2
             if tile_exists(i):
                 squared_deviations(i)
             if tile_exists(i - 3) and not handed_over(i - 3):
-                scale_and_shift(i - 3)
-                store(i - 3)
+                for cols in [half(0), half(1)] if i - 3 == N_TILES - 1 else [slice(0, H)]:
+                    scale_and_shift(i - 3, cols)
+                    store(i - 3, cols)
             if handed_over(i - 4):
                 shift_only(i - 4)
-                store(i - 4)
+                store(i - 4, slice(0, H))
             if i % GROUP == GROUP - 2 and tile_exists(i + 2):
-                quantise_ff((i + 2) // GROUP)
+                quantise_ff((i + 2) // GROUP, 0, GROUP)

@@ -236,7 +236,7 @@ def tile_disentangledattention_pc_t_kernel(tc, ff, attn_out, Wf, b_f, ln2_g, ln2
             return 0 <= i < N_TILES
 
         def handed_over(i):
-            return tile_exists(i) and i % HAND_OVER == 0
+            return tile_exists(i) and i % HAND_OVER == 1
 
         for i in range(N_TILES + 4):
             if tile_exists(i + FF_AHEAD):
@@ -258,6 +258,9 @@ def tile_disentangledattention_pc_t_kernel(tc, ff, attn_out, Wf, b_f, ln2_g, ln2
                 centre_and_gain(i - 2)
             if tile_exists(i):
                 add_residual(i, 1)
+            if i % GROUP == GROUP - 2 and tile_exists(i + 2):
+                quantise_ff((i + 2) // GROUP, 0, GROUP)
+            if tile_exists(i):
                 mean(i)
             if tile_exists(i - 1):
                 inverse_deviation(i - 1)
@@ -270,5 +273,3 @@ def tile_disentangledattention_pc_t_kernel(tc, ff, attn_out, Wf, b_f, ln2_g, ln2
             if handed_over(i - 4):
                 shift_only(i - 4)
                 store(i - 4, slice(0, H))
-            if i % GROUP == GROUP - 2 and tile_exists(i + 2):
-                quantise_ff((i + 2) // GROUP, 0, GROUP)

from contextlib import ExitStack

import concourse.mybir as mybir
from concourse.masks import make_identity

F32 = mybir.dt.float32
BF16 = mybir.dt.bfloat16
I32 = mybir.dt.int32
U32 = mybir.dt.uint32
U8 = mybir.dt.uint8
FP8X4 = mybir.dt.float8_e4m3fn_x4
ALU = mybir.AluOpType
ACT = mybir.ActivationFunctionType

P = 128
PACK = 4
K_PASS = P * PACK
TOKENS, K, H = 8 * 512, 1024, 1024
PASSES = K // K_PASS
N_TILES = TOKENS // P
GROUP = 4
BANK = 512
HALVES = H // BANK
EPS = 1e-7

FLOPS = 2 * TOKENS * K * H
PREP = GROUP + 2
FF_AHEAD = PREP + 4
RES_AHEAD = 4
HAND_OVER = 4


def tile_disentangledattention_pc_t_kernel(tc, ff, attn_out, Wf, b_f, ln2_g, ln2_b, out):
    nc = tc.nc
    ff_v = ff.rearrange("b s f -> (b s) f").rearrange("(i p) f -> i p f", p=P)
    res_v = attn_out.rearrange("b s f -> (b s) f").rearrange("(i p) f -> i p f", p=P)
    out_v = out.rearrange("b s f -> (b s) f").rearrange("(i p) f -> i p f", p=P)
    w_v = Wf.rearrange("(c q e) n -> c q e n", q=P, e=2)

    with ExitStack() as ctx:
        const = ctx.enter_context(tc.tile_pool(name="const", bufs=1))
        weights = ctx.enter_context(tc.tile_pool(name="weights", bufs=1))
        ff_pool = ctx.enter_context(tc.tile_pool(name="ff_pool", bufs=FF_AHEAD))
        res_pool = ctx.enter_context(tc.tile_pool(name="res_pool", bufs=RES_AHEAD + 1))
        quant = ctx.enter_context(tc.tile_pool(name="quant", bufs=2))
        work = ctx.enter_context(tc.tile_pool(name="work", bufs=4))
        y_pool = ctx.enter_context(tc.tile_pool(name="y_pool", bufs=6))
        stats = ctx.enter_context(tc.tile_pool(name="stats", bufs=4))
        psum_const = ctx.enter_context(tc.psum_pool(name="psum_const", bufs=1))
        psum_t = ctx.enter_context(tc.psum_pool(name="psum_t", bufs=2))
        psum_acc = ctx.enter_context(tc.psum_pool(name="psum_acc", bufs=4))
        ctx.enter_context(tc.manual_schedule())

        def half(h):
            return slice(h * BANK, (h + 1) * BANK)

        ff_sb, res_sb, xt, grouped, codes = {}, {}, {}, {}, {}
        rb, acc, u, negmean, ssq, rstd, y = {}, {}, {}, {}, {}, {}, {}

        def load_ff(i):
            ff_sb[i] = ff_pool.tile([P, K], BF16, name="ff_sb")
            nc.sync.dma_start(out=ff_sb[i][:], in_=ff_v[i])

        def load_res(i):
            res_sb[i] = res_pool.tile([P, H], BF16, name="res_sb")
            nc.sync.dma_start(out=res_sb[i][:], in_=res_v[i])

        def transpose(i):
            words = ff_sb[i][:].bitcast(F32)
            xt[i] = psum_t.tile([P, PASSES * 2, P], F32, name="xt")
            for c in range(PASSES * 2):
                nc.tensor.transpose(xt[i][:, c, :], words[:, c * P : (c + 1) * P], ident[:])

        def regroup(i):
            if i % GROUP == 0:
                grouped[i // GROUP] = quant.tile([P, GROUP, PASSES, P, PACK], BF16, align_bytes=64, name="grouped")
            nc.scalar.copy(
                out=grouped[i // GROUP][:, i % GROUP].bitcast(F32),
                in_=xt[i][:].rearrange("p (g u) r -> p g r u", u=2),
            )

        def quantise_ff(n, first, count):
            if first == 0:
                ff_codes = quant.tile([P, GROUP * PASSES * P], U32, align_bytes=64)
                ff_scales = quant.tile([P, GROUP * PASSES * P], U8, align_bytes=64)
                codes[n] = (ff_codes, ff_scales)
            ff_codes, ff_scales = codes[n]
            words = slice(first * PASSES * P, (first + count) * PASSES * P)
            nc.vector.quantize_mx(
                out=ff_codes[:, words].bitcast(FP8X4),
                scales=ff_scales[:, words],
                in_=grouped[n][:, first : first + count].rearrange("p j g r t -> p (j g r t)"),
            )

        def add_bias(i):
            rb[i] = work.tile([P, H], F32, name="rb")
            nc.gpsimd.tensor_tensor(out=rb[i][:], in0=res_sb[i][:], in1=bias_bc[:], op=ALU.add)

        def project(i):
            ff_codes, ff_scales = codes[i // GROUP]
            for h in range(HALVES):
                acc[i, h] = psum_acc.tile([P, BANK], F32, name="acc")
                for g in range(PASSES):
                    tok = slice(((i % GROUP) * PASSES + g) * P, ((i % GROUP) * PASSES + g + 1) * P)
                    nc.tensor.matmul_mx(
                        out=acc[i, h][:],
                        lhsT=ff_codes[:, tok].bitcast(FP8X4),
                        lhsT_scale=ff_scales[:, tok],
                        rhs=w_codes[:, g, half(h)].bitcast(FP8X4),
                        rhs_scale=w_scales[:, g, half(h)],
                        start=(g == 0),
                        stop=(g == PASSES - 1),
                    )

        def add_residual(i, h):
            if h == 0:
                u[i] = work.tile([P, H], F32, name="u")
            nc.vector.tensor_tensor(out=u[i][:, half(h)], in0=acc[i, h][:], in1=rb[i][:, half(h)], op=ALU.add)

        def mean(i):
            negmean[i] = stats.tile([P, 1], F32, name="negmean")
            unused = stats.tile([P, H], BF16, name="unused")
            nc.scalar.activation(out=unused[:], in_=u[i][:], func=ACT.Identity, scale=-1.0 / H, accum_out=negmean[i][:])

        def squared_deviations(i):
            ssq[i] = stats.tile([P, 1], F32, name="ssq")
            unused = stats.tile([P, H], BF16, name="unused")
            nc.scalar.activation(out=unused[:], in_=u[i][:], func=ACT.Square, bias=negmean[i][:], scale=1.0, accum_out=ssq[i][:])

        def inverse_deviation(i):
            rstd[i] = stats.tile([P, 1], F32, name="rstd")
            nc.scalar.activation(out=rstd[i][:], in_=ssq[i][:], func=ACT.Abs_reciprocal_sqrt, bias=eps_t[:], scale=1.0 / H)

        def centre_and_gain(i):
            y[i] = y_pool.tile([P, H], F32, name="y")
            nc.vector.scalar_tensor_tensor(out=y[i][:], in0=u[i][:], scalar=negmean[i][:], in1=gain_ps[:], op0=ALU.add, op1=ALU.mult)

        def scale_and_shift(i, cols):
            nc.vector.scalar_tensor_tensor(out=y[i][:, cols], in0=y[i][:, cols], scalar=rstd[i][:], in1=shift_ps[:, cols], op0=ALU.mult, op1=ALU.add)

        def scale_only(i):
            nc.scalar.activation(out=y[i][:], in_=y[i][:], func=ACT.Copy, scale=rstd[i][:])

        def shift_only(i):
            nc.gpsimd.tensor_tensor(out=y[i][:], in0=y[i][:], in1=shift_bc[:], op=ALU.add)

        def store(i, cols):
            nc.sync.dma_start(out=out_v[i][:, cols], in_=y[i][:, cols])

        ident = const.tile([P, P], F32)
        make_identity(nc, ident[:])
        ones = const.tile([P, P], BF16)
        nc.vector.memset(ones[:], 1.0)
        rows = {}
        for name in ("bias", "gain", "shift"):
            rows[name] = const.tile([P, H], BF16, name="row_" + name)
            nc.vector.memset(rows[name][:].bitcast(I32), 0)
        eps_t = const.tile([P, 1], F32)
        nc.vector.memset(eps_t[:], EPS)
        warm = const.tile([P, 1], F32)
        nc.scalar.activation(out=warm[:], in_=eps_t[:], func=ACT.Abs_reciprocal_sqrt)

        def load_row(name, vec):
            nc.sync.dma_start(out=rows[name][0:1, :], in_=vec.rearrange("(o n) -> o n", o=1))

        def spread_row(name, h, out_ps):
            nc.tensor.matmul(out=out_ps, lhsT=ones[:], rhs=rows[name][:, half(h)], start=True, stop=True)

        w_raw = weights.tile([P, PASSES, PACK, H], BF16)

        def load_w(g, h):
            for u2 in range(2):
                nc.sync.dma_start(out=w_raw[:, g, 2 * u2 : 2 * u2 + 2, half(h)], in_=w_v[2 * g + u2][:, :, half(h)])

        load_w(0, 0)
        load_row("bias", b_f)
        load_w(1, 0)
        load_w(0, 1)
        load_w(1, 1)
        for i in range(RES_AHEAD):
            load_ff(i)
            load_res(i)
        load_row("gain", ln2_g)
        load_row("shift", ln2_b)
        for i in range(RES_AHEAD, FF_AHEAD):
            load_ff(i)

        bias_bc = const.tile([P, H], BF16)
        for h in range(HALVES):
            bias_ps = psum_acc.tile([P, BANK], F32, name="acc")
            spread_row("bias", h, bias_ps[:])
            nc.scalar.copy(out=bias_bc[:, half(h)], in_=bias_ps[:])
        add_bias(0)

        w_grp = weights.tile([P, PASSES, H, PACK], BF16, align_bytes=64)
        w_codes = weights.tile([P, PASSES, H], U32, align_bytes=64)
        w_scales = weights.tile([P, PASSES, H], U8, align_bytes=64)

        def regroup_w(g, h):
            nc.vector.tensor_copy(
                out=w_grp[:, g, half(h), :].rearrange("p (c i) t -> p c t i", i=4),
                in_=w_raw[:, g, :, half(h)].rearrange("p t (c i) -> p c t i", i=4),
            )

        def quantise_w(g, h):
            nc.vector.quantize_mx(
                out=w_codes[:, g, half(h)].bitcast(FP8X4),
                scales=w_scales[:, g, half(h)],
                in_=w_grp[:, g, half(h), :].rearrange("p n t -> p (n t)"),
            )

        for h in range(HALVES):
            for g in range(PASSES):
                regroup_w(g, h)
            for g in range(PASSES):
                quantise_w(g, h)

        for i in range(GROUP):
            transpose(i)
            regroup(i)
            quantise_ff(0, i, 1)

        gain_ps = psum_const.tile([P, H], BF16)
        shift_ps = psum_const.tile([P, H], BF16)
        for h in range(HALVES):
            spread_row("gain", h, gain_ps[:, half(h)])
            spread_row("shift", h, shift_ps[:, half(h)])
        shift_bc = const.tile([P, H], BF16)
        nc.scalar.copy(out=shift_bc[:], in_=shift_ps[:])

        for i in range(GROUP, PREP):
            transpose(i)
            regroup(i)

        def tile_exists(i):
            return 0 <= i < N_TILES

        def handed_over(i):
            return tile_exists(i) and i % HAND_OVER == 1

        for i in range(N_TILES + 4):
            if tile_exists(i + FF_AHEAD):
                load_ff(i + FF_AHEAD)
            if tile_exists(i + RES_AHEAD):
                load_res(i + RES_AHEAD)
            if tile_exists(i + 1):
                add_bias(i + 1)
            if tile_exists(i):
                project(i)
            if tile_exists(i + PREP):
                transpose(i + PREP)
                regroup(i + PREP)
            if handed_over(i - 3):
                scale_only(i - 3)
            if tile_exists(i):
                add_residual(i, 0)
            if tile_exists(i - 2):
                centre_and_gain(i - 2)
            if tile_exists(i):
                add_residual(i, 1)
            if i % GROUP == GROUP - 2 and tile_exists(i + 2):
                quantise_ff((i + 2) // GROUP, 0, GROUP)
            if tile_exists(i):
                mean(i)
            if tile_exists(i - 1):
                inverse_deviation(i - 1)
            if tile_exists(i):
                squared_deviations(i)
            if tile_exists(i - 3) and not handed_over(i - 3):
                for cols in [half(0), half(1)] if i - 3 == N_TILES - 1 else [slice(0, H)]:
                    scale_and_shift(i - 3, cols)
                    store(i - 3, cols)
            if handed_over(i - 4):
                shift_only(i - 4)
                store(i - 4, slice(0, H))
